import numpy as np
import ml_dtypes


def mxq(x, axis, fmt="e4m3"):
    dtype, down = {"e4m3": (ml_dtypes.float8_e4m3fn, 7), "e5m2": (ml_dtypes.float8_e5m2, 14)}[fmt]
    v = np.moveaxis(np.asarray(x, np.float32).astype(ml_dtypes.bfloat16).astype(np.float64), axis, -1)
    blocks = v.reshape(v.shape[:-1] + (-1, 32))
    amax = np.abs(blocks).max(-1, keepdims=True)
    byte = np.maximum(np.where(amax > 0, np.frexp(amax)[1] - 1 + 127, 0) - down, 1)
    scale = np.exp2(byte - 127.0)
    codes = (blocks / scale).astype(np.float32).astype(dtype).astype(np.float64)
    return np.moveaxis((codes * scale).reshape(v.shape), -1, axis)


WIDE = False


def mx_kscale(k):
    if not WIDE:
        return np.ones(k)
    levels = np.array([10, -10, 5, -5, 0])
    a = np.random.permutation(np.resize(levels, k // 512 * 4)).reshape(k // 512, 4)
    idx = np.arange(k)
    return np.exp2(a[idx // 512, idx % 128 // 32])


BF16 = ml_dtypes.bfloat16


def bf(x):
    return np.asarray(x, np.float32).astype(BF16)


def f64(x):
    return np.asarray(x).astype(np.float64)


B, SI, ST, DM, H, D = 4, 1536, 512, 1024, 1, 128
S = ST + SI
HD = H * D
EPS = 1e-6


def rms_norm(x, gamma):
    var = np.mean(x * x, axis=-1, keepdims=True)
    return x * (1.0 / np.sqrt(var + EPS)) * gamma


def apply_rotary(x, cos, sin):
    xr = x.reshape(B, S, H, D // 2, 2)
    x1, x2 = xr[..., 0], xr[..., 1]
    rot = np.stack([-x2, x1], axis=-1).reshape(B, S, H, D)
    return x * cos[None, :, None, :] + rot * sin[None, :, None, :]


def heads(y):
    return y.reshape(B, -1, H, D)


def setup_inputs():
    s = mx_kscale(DM)
    w = 1.0 / np.sqrt(DM)
    pos = np.arange(S)[:, None]
    inv = 1.0 / (10000.0 ** (np.arange(0, D, 2) / D))
    ang = np.repeat(pos * inv[None, :], 2, axis=-1)
    inp = {"hidden_states": bf(np.random.standard_normal((B, SI, DM)) * s),
           "encoder_hidden_states": bf(np.random.standard_normal((B, ST, DM)) * s),
           "rope_cos": bf(np.cos(ang)), "rope_sin": bf(np.sin(ang))}
    for n in ["Wq", "Wk", "Waq", "Wak"]:
        inp[n] = bf(np.random.standard_normal((DM, HD)) * w / s[:, None])
    for n in ["bq", "bk", "baq", "bak"]:
        inp[n] = bf(np.random.standard_normal(HD) * 0.3)
    for n in ["g_q", "g_k", "g_aq", "g_ak"]:
        inp[n] = bf(1.5 * (1.0 + 0.1 * np.random.standard_normal(D)))
    return inp


def reference(hidden_states, encoder_hidden_states, rope_cos, rope_sin, Wq, bq, Wk, bk, Waq, baq, Wak, bak, g_q, g_k, g_aq, g_ak):
    xq = mxq(f64(hidden_states), 2, "e4m3")
    cq = mxq(f64(encoder_hidden_states), 2, "e4m3")
    q = rms_norm(heads((xq @ mxq(f64(Wq), 0, "e4m3")) + f64(bq)), f64(g_q))
    k = rms_norm(heads((xq @ mxq(f64(Wk), 0, "e4m3")) + f64(bk)), f64(g_k))
    eq = rms_norm(heads((cq @ mxq(f64(Waq), 0, "e4m3")) + f64(baq)), f64(g_aq))
    ek = rms_norm(heads((cq @ mxq(f64(Wak), 0, "e4m3")) + f64(bak)), f64(g_ak))
    q = np.concatenate([eq, q], axis=1)
    k = np.concatenate([ek, k], axis=1)
    return apply_rotary(q, f64(rope_cos), f64(rope_sin)), apply_rotary(k, f64(rope_cos), f64(rope_sin))

@@ -1,0 +1,319 @@
+from contextlib import ExitStack
+
+import concourse.mybir as mybir
+from concourse.masks import make_identity
+
+F32 = mybir.dt.float32
+BF16 = mybir.dt.bfloat16
+U32 = mybir.dt.uint32
+U8 = mybir.dt.uint8
+FP8X4 = mybir.dt.float8_e4m3fn_x4
+ACT = mybir.ActivationFunctionType
+ALU = mybir.AluOpType
+
+P = 128
+BATCH = 4
+K = 1024
+D = 128
+HALF = D // 2
+EPS = 1e-6
+BLOCK = 512
+T = BLOCK // P
+BLOCKS = 4
+GROUPS = BLOCKS * BATCH
+PASSES = K // 512
+WORD_TILES = K // 2 // P
+LOOKAHEAD = 4
+
+FLOPS = 2 * BATCH * BLOCKS * BLOCK * K * 2 * D
+
+
+def tile_fluxjointattention_pa_t_kernel(
+    tc,
+    hidden_states,
+    encoder_hidden_states,
+    rope_cos,
+    rope_sin,
+    Wq,
+    Wk,
+    Waq,
+    Wak,
+    bq,
+    bk,
+    baq,
+    bak,
+    g_q,
+    g_k,
+    g_aq,
+    g_ak,
+    out_0,
+    out_1,
+):
+    nc = tc.nc
+    outs = (out_0, out_1)
+    weights = (Waq, Wak, Wq, Wk)
+    biases = (baq, bak, bq, bk)
+    gains = (g_aq, g_ak, g_q, g_k)
+
+    with ExitStack() as ctx:
+        consts = ctx.enter_context(tc.tile_pool(name="consts", bufs=1))
+        work = ctx.enter_context(tc.tile_pool(name="work", bufs=2))
+        psum = ctx.enter_context(tc.psum_pool(name="psum", bufs=1))
+
+        x_tiles = {}
+        grouped_tiles = {}
+        mx_tiles = {}
+        yt_tiles = {}
+        ybt_tiles = {}
+        ybp_tiles = {}
+        r_tiles = {}
+
+        def load_x(g):
+            block, b = divmod(g, BATCH)
+            if block == 0:
+                rows = encoder_hidden_states[b]
+            else:
+                rows = hidden_states[b, (block - 1) * BLOCK : block * BLOCK, :]
+            x_sb = work.tile([P, T * K], BF16, tag="x", bufs=LOOKAHEAD + 2)
+            nc.sync.dma_start(out=x_sb[:], in_=rows.rearrange("(p t) k -> p (t k)", t=T))
+            x_tiles[g] = x_sb
+
+        warm = consts.tile([P, 1], F32)
+        nc.vector.memset(warm[:], 1.0)
+        nc.scalar.activation(out=warm[:], in_=warm[:], func=ACT.Sqrt)
+
+        bias_rows = consts.tile([P, P], BF16)
+        nc.vector.memset(bias_rows[:], 0.0)
+        gain_rows = consts.tile([P, 4 * D], BF16)
+        nc.vector.memset(gain_rows[:], 0.0)
+        ones = consts.tile([P, P], BF16)
+        nc.vector.memset(ones[:], 1.0)
+
+        ident = consts.tile([P, P], F32)
+        make_identity(nc, ident[:])
+        ident_bf = consts.tile([P, P], BF16)
+        nc.vector.tensor_copy(out=ident_bf[:], in_=ident[:])
+        split = consts.tile([P, D], F32)
+        nc.vector.tensor_copy(
+            out=split[:].rearrange("p (h i) -> p h i", h=2),
+            in_=ident[:].rearrange("p (i h) -> p h i", h=2),
+        )
+
+        w_raw = {}
+
+        def load_weights(stream):
+            raw = consts.tile([P, 2 * K * D // P], BF16, name="w_raw%d" % stream)
+            for qk in range(2):
+                nc.sync.dma_start(
+                    out=raw[:, qk * 1024 : (qk + 1) * 1024].rearrange("p (a f) -> p a f", a=4),
+                    in_=weights[2 * stream + qk].rearrange("(a p e) n -> p a (e n)", a=4, p=P, e=2),
+                )
+            w_raw[stream] = raw
+
+        load_x(0)
+        load_weights(0)
+        for j in range(4):
+            nc.sync.dma_start(out=bias_rows[j : j + 1, :], in_=biases[j].unsqueeze(0))
+            nc.sync.dma_start(out=gain_rows[0:1, j * D : (j + 1) * D], in_=gains[j].unsqueeze(0))
+        load_x(1)
+        cos_sb = consts.tile([P, BLOCKS, T * D], BF16)
+        nc.sync.dma_start(out=cos_sb[:], in_=rope_cos.rearrange("(c p t) d -> p c (t d)", c=BLOCKS, p=P, t=T))
+        sin_sb = consts.tile([P, BLOCKS, T * D], BF16)
+        nc.sync.dma_start(out=sin_sb[:], in_=rope_sin.rearrange("(c p t) d -> p c (t d)", c=BLOCKS, p=P, t=T))
+        load_x(2)
+        load_x(3)
+        load_weights(1)
+
+        w_codes = {}
+        w_scales = {}
+
+        def quantise_weights(stream):
+            grouped = consts.tile([P, 2048], BF16, name="w_grouped%d" % stream, align_bytes=64)
+            nc.vector.tensor_copy(
+                out=grouped[:].rearrange("p (m n j) -> p m n j", m=4, j=4),
+                in_=w_raw[stream][:].rearrange("p (m j n) -> p m n j", m=4, j=4),
+            )
+            codes = consts.tile([P, 512], U32, name="w_codes%d" % stream, align_bytes=64)
+            scales = consts.tile([P, 512], U8, name="w_scales%d" % stream, align_bytes=64)
+            nc.vector.quantize_mx(out=codes[:].bitcast(FP8X4), scales=scales[:], in_=grouped[:])
+            w_codes[stream] = codes
+            w_scales[stream] = scales
+
+        bias_col = consts.tile([P, 4], F32)
+        gain_cos = consts.tile([P, 4, 2, HALF], F32)
+        gain_sin = consts.tile([P, 4, 2, HALF], F32)
+
+        def spread_vectors():
+            bias_ps = psum.tile([P, P], BF16, tag="ybp", bufs=3)
+            nc.tensor.transpose(bias_ps[:], bias_rows[:], ident_bf[:])
+            nc.vector.tensor_copy(out=bias_col[:], in_=bias_ps[:, 0:4])
+            gain_ps = psum.tile([P, 4 * D], F32, tag="yt", bufs=2)
+            nc.tensor.matmul(out=gain_ps[:], lhsT=ones[:], rhs=gain_rows[:], start=True, stop=True)
+            nc.vector.tensor_copy(out=gain_cos[:], in_=gain_ps[:].rearrange("p (j i h) -> p j h i", j=4, h=2))
+            nc.vector.tensor_copy(out=gain_sin[:, :, 0, :], in_=gain_cos[:, :, 0, :])
+            nc.vector.tensor_scalar_mul(out=gain_sin[:, :, 1, :], in0=gain_cos[:, :, 1, :], scalar1=-1.0)
+
+        cos_tabs = {}
+        sin_tabs = {}
+
+        def build_tables(block, qk):
+            j = 2 * min(block, 1) + qk
+            cos_tab = consts.tile([P, T, D], F32, name="cos_tab%d_%d" % (block, qk))
+            nc.gpsimd.tensor_tensor(
+                out=cos_tab[:].rearrange("p t (h i) -> p t h i", h=2),
+                in0=cos_sb[:, block, :].rearrange("p (t i h) -> p t h i", t=T, h=2),
+                in1=gain_cos[:, j].unsqueeze(1).to_broadcast([P, T, 2, HALF]),
+                op=ALU.mult,
+            )
+            sin_tab = consts.tile([P, T, 2, HALF], F32, name="sin_tab%d_%d" % (block, qk))
+            sin_pairs = sin_sb[:, block, :].rearrange("p (t i h) -> p t h i", t=T, h=2)
+            for h in range(2):
+                nc.gpsimd.tensor_tensor(
+                    out=sin_tab[:, :, h, :],
+                    in0=sin_pairs[:, :, 1 - h, :],
+                    in1=gain_sin[:, j, h, :].unsqueeze(1).to_broadcast([P, T, HALF]),
+                    op=ALU.mult,
+                )
+            cos_tabs[(block, qk)] = cos_tab
+            sin_tabs[(block, qk)] = sin_tab
+
+        def transpose_x(g):
+            x_words = x_tiles[g][:].bitcast(F32)
+            grouped = work.tile([P, PASSES * BLOCK * 4], BF16, tag="grouped", bufs=2, align_bytes=64)
+            grouped_words = grouped[:].bitcast(F32).rearrange("p (c n u) -> p c n u", c=PASSES, u=2)
+            for t in range(T):
+                xt = psum.tile([P, WORD_TILES, P], F32, tag="xt", bufs=3)
+                for a in range(WORD_TILES):
+                    first = t * (K // 2) + a * P
+                    nc.tensor.transpose(xt[:, a, :], x_words[:, first : first + P], ident[:])
+                copy_out = nc.vector.tensor_copy if t == 0 else nc.scalar.copy
+                copy_out(
+                    out=grouped_words[:, :, t * P : (t + 1) * P, :],
+                    in_=xt[:].rearrange("p (c u) n -> p c n u", c=PASSES),
+                )
+            grouped_tiles[g] = grouped
+
+        def quantise_x(g):
+            grouped = grouped_tiles[g]
+            codes = work.tile([P, PASSES * BLOCK], U32, tag="codes", bufs=2, align_bytes=64)
+            scales = work.tile([P, PASSES * BLOCK], U8, tag="scales", bufs=2, align_bytes=64)
+            nc.vector.quantize_mx(out=codes[:].bitcast(FP8X4), scales=scales[:], in_=grouped[:])
+            mx_tiles[g] = (codes, scales)
+
+        def project(g):
+            stream = min(g // BATCH, 1)
+            codes, scales = mx_tiles[g]
+            for qk in range(2):
+                yt = psum.tile([P, BLOCK], F32, tag="yt", bufs=2)
+                for c in range(PASSES):
+                    w_cols = slice((2 * qk + c) * P, (2 * qk + c + 1) * P)
+                    x_cols = slice(c * BLOCK, (c + 1) * BLOCK)
+                    nc.tensor.matmul_mx(
+                        out=yt[:],
+                        lhsT=w_codes[stream][:, w_cols].bitcast(FP8X4),
+                        lhsT_scale=w_scales[stream][:, w_cols],
+                        rhs=codes[:, x_cols].bitcast(FP8X4),
+                        rhs_scale=scales[:, x_cols],
+                        start=(c == 0),
+                        stop=(c == PASSES - 1),
+                    )
+                yt_tiles[(g, qk)] = yt
+
+        def add_bias(g):
+            stream = min(g // BATCH, 1)
+            for qk in range(2):
+                ybt = work.tile([P, BLOCK], F32, tag="ybt", bufs=4)
+                j = 2 * stream + qk
+                nc.scalar.activation(
+                    out=ybt[:], in_=yt_tiles[(g, qk)][:], func=ACT.Identity, bias=bias_col[:, j : j + 1]
+                )
+                ybt_tiles[(g, qk)] = ybt
+
+        def transpose_back(g):
+            for qk in range(2):
+                ybt = ybt_tiles[(g, qk)]
+                ybp = psum.tile([P, T, D], F32, tag="ybp", bufs=3)
+                for t in range(T):
+                    nc.tensor.transpose(ybp[:, t, :], ybt[:, t * P : (t + 1) * P], split[:])
+                ybp_tiles[(g, qk)] = ybp
+
+        def norms(g):
+            ss = work.tile([P, 2 * T], F32, tag="ss", bufs=3)
+            for qk in range(2):
+                for t in range(T):
+                    squares = work.tile([P, D], F32, tag="squares", bufs=2)
+                    nc.scalar.activation(
+                        out=squares[:],
+                        in_=ybp_tiles[(g, qk)][:, t, :],
+                        func=ACT.Square,
+                        accum_out=ss[:, qk * T + t : qk * T + t + 1],
+                    )
+            rms = work.tile([P, 2 * T], F32, tag="rms", bufs=3)
+            nc.scalar.activation(out=rms[:], in_=ss[:], func=ACT.Sqrt, scale=1.0 / D, bias=EPS)
+            r = work.tile([P, 2 * T], F32, tag="r", bufs=3)
+            nc.vector.reciprocal(out=r[:], in_=rms[:])
+            r_tiles[g] = r
+
+        def rotate_and_store(g):
+            block, b = divmod(g, BATCH)
+            r = r_tiles[g]
+            for qk in range(2):
+                ybp = ybp_tiles[(g, qk)]
+                planes = work.tile([P, T, 4, HALF], F32, tag="planes%d" % qk, bufs=3)
+                for t in range(T):
+                    col = qk * T + t
+                    halves = ybp[:, t, :].rearrange("p (h i) -> p h i", h=2)
+                    nc.vector.scalar_tensor_tensor(
+                        out=planes[:, t, 0:4:3, :],
+                        in0=halves,
+                        scalar=r[:, col : col + 1],
+                        in1=cos_tabs[(block, qk)][:, t, :].rearrange("p (h i) -> p h i", h=2),
+                        op0=ALU.mult,
+                        op1=ALU.mult,
+                    )
+                    nc.vector.scalar_tensor_tensor(
+                        out=planes[:, t, 1:3, :],
+                        in0=halves,
+                        scalar=r[:, col : col + 1],
+                        in1=sin_tabs[(block, qk)][:, t, :, :],
+                        op0=ALU.mult,
+                        op1=ALU.mult,
+                    )
+                result = work.tile([P, T, D], F32, tag="result%d" % qk, bufs=3)
+                nc.gpsimd.tensor_tensor(
+                    out=result[:].rearrange("p t (i h) -> p t i h", h=2),
+                    in0=planes[:, :, 0:2, :].rearrange("p t h i -> p t i h"),
+                    in1=planes[:, :, 2:4, :].rearrange("p t h i -> p t i h"),
+                    op=ALU.add,
+                )
+                nc.sync.dma_start(
+                    out=outs[qk][b, block * BLOCK : (block + 1) * BLOCK, 0, :].rearrange("(p t) d -> p t d", t=T),
+                    in_=result[:],
+                )
+
+        for i in range(GROUPS + 3):
+            if i + LOOKAHEAD < GROUPS:
+                load_x(i + LOOKAHEAD)
+            if 0 <= i - 2 < GROUPS:
+                add_bias(i - 2)
+            if i < GROUPS:
+                transpose_x(i)
+            if i == 0:
+                spread_vectors()
+                quantise_weights(0)
+                for qk in range(2):
+                    build_tables(0, qk)
+            if i == 3:
+                quantise_weights(1)
+            if 0 <= i - 3 < GROUPS:
+                rotate_and_store(i - 3)
+            if i % BATCH < 2 and i // BATCH + 1 < BLOCKS:
+                build_tables(i // BATCH + 1, i % BATCH)
+            if 0 <= i - 2 < GROUPS:
+                transpose_back(i - 2)
+            if 0 <= i - 1 < GROUPS:
+                project(i - 1)
+            if i < GROUPS:
+                quantise_x(i)
+            if 0 <= i - 2 < GROUPS:
+                norms(i - 2)

@@ -93,11 +93,6 @@ def tile_fluxjointattention_pa_t_kernel(
         make_identity(nc, ident[:])
         ident_bf = consts.tile([P, P], BF16)
         nc.vector.tensor_copy(out=ident_bf[:], in_=ident[:])
-        split = consts.tile([P, D], F32)
-        nc.vector.tensor_copy(
-            out=split[:].rearrange("p (h i) -> p h i", h=2),
-            in_=ident[:].rearrange("p (i h) -> p h i", h=2),
-        )
 
         w_raw = {}
 
@@ -140,8 +135,7 @@ def tile_fluxjointattention_pa_t_kernel(
             w_scales[stream] = scales
 
         bias_col = consts.tile([P, 4], F32)
-        gain_cos = consts.tile([P, 4, 2, HALF], F32)
-        gain_sin = consts.tile([P, 4, 2, HALF], F32)
+        gain_pairs = consts.tile([P, 4, 3, HALF], F32)
 
         def spread_vectors():
             bias_ps = psum.tile([P, P], BF16, tag="ybp", bufs=3)
@@ -149,33 +143,34 @@ def tile_fluxjointattention_pa_t_kernel(
             nc.vector.tensor_copy(out=bias_col[:], in_=bias_ps[:, 0:4])
             gain_ps = psum.tile([P, 4 * D], F32, tag="yt", bufs=2)
             nc.tensor.matmul(out=gain_ps[:], lhsT=ones[:], rhs=gain_rows[:], start=True, stop=True)
-            nc.vector.tensor_copy(out=gain_cos[:], in_=gain_ps[:].rearrange("p (j i h) -> p j h i", j=4, h=2))
-            nc.vector.tensor_copy(out=gain_sin[:, :, 0, :], in_=gain_cos[:, :, 0, :])
-            nc.vector.tensor_scalar_mul(out=gain_sin[:, :, 1, :], in0=gain_cos[:, :, 1, :], scalar1=-1.0)
+            nc.vector.tensor_copy(
+                out=gain_pairs[:, :, 0:2, :], in_=gain_ps[:].rearrange("p (j i h) -> p j h i", j=4, h=2)
+            )
+            nc.vector.tensor_scalar_mul(out=gain_pairs[:, :, 2, :], in0=gain_pairs[:, :, 1, :], scalar1=-1.0)
 
-        cos_tabs = {}
-        sin_tabs = {}
+        even_tabs = {}
+        odd_tabs = {}
 
         def build_tables(block, qk):
             j = 2 * min(block, 1) + qk
-            cos_tab = consts.tile([P, T, D], F32, name="cos_tab%d_%d" % (block, qk))
-            nc.gpsimd.tensor_tensor(
-                out=cos_tab[:].rearrange("p t (h i) -> p t h i", h=2),
-                in0=cos_sb[:, block, :].rearrange("p (t i h) -> p t h i", t=T, h=2),
-                in1=gain_cos[:, j].unsqueeze(1).to_broadcast([P, T, 2, HALF]),
-                op=ALU.mult,
-            )
-            sin_tab = consts.tile([P, T, 2, HALF], F32, name="sin_tab%d_%d" % (block, qk))
+            cos_pairs = cos_sb[:, block, :].rearrange("p (t i h) -> p t h i", t=T, h=2)
             sin_pairs = sin_sb[:, block, :].rearrange("p (t i h) -> p t h i", t=T, h=2)
-            for h in range(2):
+            even_tab = consts.tile([P, T, 2, HALF], F32, name="even_tab%d_%d" % (block, qk))
+            odd_tab = consts.tile([P, T, 2, HALF], F32, name="odd_tab%d_%d" % (block, qk))
+            for table, h, angles, gain in (
+                (even_tab, 0, cos_pairs, 0),
+                (even_tab, 1, sin_pairs, 0),
+                (odd_tab, 0, sin_pairs, 2),
+                (odd_tab, 1, cos_pairs, 1),
+            ):
                 nc.gpsimd.tensor_tensor(
-                    out=sin_tab[:, :, h, :],
-                    in0=sin_pairs[:, :, 1 - h, :],
-                    in1=gain_sin[:, j, h, :].unsqueeze(1).to_broadcast([P, T, HALF]),
+                    out=table[:, :, h, :],
+                    in0=angles[:, :, h, :],
+                    in1=gain_pairs[:, j, gain, :].unsqueeze(1).to_broadcast([P, T, HALF]),
                     op=ALU.mult,
                 )
-            cos_tabs[(block, qk)] = cos_tab
-            sin_tabs[(block, qk)] = sin_tab
+            even_tabs[(block, qk)] = even_tab
+            odd_tabs[(block, qk)] = odd_tab
 
         def transpose_x(g):
             x_words = x_tiles[g][:].bitcast(F32)
@@ -234,7 +229,7 @@ def tile_fluxjointattention_pa_t_kernel(
                 ybt = ybt_tiles[(g, qk)]
                 ybp = psum.tile([P, T, D], F32, tag="ybp", bufs=3)
                 for t in range(T):
-                    nc.tensor.transpose(ybp[:, t, :], ybt[:, t * P : (t + 1) * P], split[:])
+                    nc.tensor.transpose(ybp[:, t, :], ybt[:, t * P : (t + 1) * P], ident[:])
                 ybp_tiles[(g, qk)] = ybp
 
         def norms(g):
@@ -259,33 +254,22 @@ def tile_fluxjointattention_pa_t_kernel(
             r = r_tiles[g]
             for qk in range(2):
                 ybp = ybp_tiles[(g, qk)]
-                planes = work.tile([P, T, 4, HALF], F32, tag="planes%d" % qk, bufs=3)
+                from_even = work.tile([P, T, D], F32, tag="from_even", bufs=4)
+                from_odd = work.tile([P, T, D], F32, tag="from_odd", bufs=4)
                 for t in range(T):
                     col = qk * T + t
-                    halves = ybp[:, t, :].rearrange("p (h i) -> p h i", h=2)
-                    nc.vector.scalar_tensor_tensor(
-                        out=planes[:, t, 0:4:3, :],
-                        in0=halves,
-                        scalar=r[:, col : col + 1],
-                        in1=cos_tabs[(block, qk)][:, t, :].rearrange("p (h i) -> p h i", h=2),
-                        op0=ALU.mult,
-                        op1=ALU.mult,
-                    )
-                    nc.vector.scalar_tensor_tensor(
-                        out=planes[:, t, 1:3, :],
-                        in0=halves,
-                        scalar=r[:, col : col + 1],
-                        in1=sin_tabs[(block, qk)][:, t, :, :],
-                        op0=ALU.mult,
-                        op1=ALU.mult,
-                    )
-                result = work.tile([P, T, D], F32, tag="result%d" % qk, bufs=3)
-                nc.gpsimd.tensor_tensor(
-                    out=result[:].rearrange("p t (i h) -> p t i h", h=2),
-                    in0=planes[:, :, 0:2, :].rearrange("p t h i -> p t i h"),
-                    in1=planes[:, :, 2:4, :].rearrange("p t h i -> p t i h"),
-                    op=ALU.add,
-                )
+                    pairs = ybp[:, t, :].rearrange("p (i h) -> p i h", h=2)
+                    for h, tabs, part in ((0, even_tabs, from_even), (1, odd_tabs, from_odd)):
+                        nc.vector.scalar_tensor_tensor(
+                            out=part[:, t, :].rearrange("p (i h) -> p i h", h=2),
+                            in0=pairs[:, :, h : h + 1].to_broadcast([P, HALF, 2]),
+                            scalar=r[:, col : col + 1],
+                            in1=tabs[(block, qk)][:, t, :, :].rearrange("p h i -> p i h"),
+                            op0=ALU.mult,
+                            op1=ALU.mult,
+                        )
+                result = work.tile([P, T, D], F32, tag="result", bufs=4)
+                nc.gpsimd.tensor_tensor(out=result[:], in0=from_even[:], in1=from_odd[:], op=ALU.add)
                 nc.sync.dma_start(
                     out=outs[qk][b, block * BLOCK : (block + 1) * BLOCK, 0, :].rearrange("(p t) d -> p t d", t=T),
                     in_=result[:],

@@ -181,8 +181,7 @@ def tile_fluxjointattention_pa_t_kernel(
                 for a in range(WORD_TILES):
                     first = t * (K // 2) + a * P
                     nc.tensor.transpose(xt[:, a, :], x_words[:, first : first + P], ident[:])
-                copy_out = nc.vector.tensor_copy if t == 0 else nc.scalar.copy
-                copy_out(
+                nc.scalar.copy(
                     out=grouped_words[:, :, t * P : (t + 1) * P, :],
                     in_=xt[:].rearrange("p (c u) n -> p c n u", c=PASSES),
                 )
@@ -269,7 +268,7 @@ def tile_fluxjointattention_pa_t_kernel(
                             op1=ALU.mult,
                         )
                 result = work.tile([P, T, D], F32, tag="result", bufs=4)
-                nc.gpsimd.tensor_tensor(out=result[:], in0=from_even[:], in1=from_odd[:], op=ALU.add)
+                nc.vector.tensor_tensor(out=result[:], in0=from_even[:], in1=from_odd[:], op=ALU.add)
                 nc.sync.dma_start(
                     out=outs[qk][b, block * BLOCK : (block + 1) * BLOCK, 0, :].rearrange("(p t) d -> p t d", t=T),
                     in_=result[:],

@@ -138,7 +138,7 @@ def tile_fluxjointattention_pa_t_kernel(
         gain_pairs = consts.tile([P, 4, 3, HALF], F32)
 
         def spread_vectors():
-            bias_ps = psum.tile([P, P], BF16, tag="ybp", bufs=3)
+            bias_ps = psum.tile([P, P], BF16, tag="ybp", bufs=2)
             nc.tensor.transpose(bias_ps[:], bias_rows[:], ident_bf[:])
             nc.vector.tensor_copy(out=bias_col[:], in_=bias_ps[:, 0:4])
             gain_ps = psum.tile([P, 4 * D], F32, tag="yt", bufs=2)
@@ -177,11 +177,12 @@ def tile_fluxjointattention_pa_t_kernel(
             grouped = work.tile([P, PASSES * BLOCK * 4], BF16, tag="grouped", bufs=2, align_bytes=64)
             grouped_words = grouped[:].bitcast(F32).rearrange("p (c n u) -> p c n u", c=PASSES, u=2)
             for t in range(T):
-                xt = psum.tile([P, WORD_TILES, P], F32, tag="xt", bufs=3)
+                xt = psum.tile([P, WORD_TILES, P], F32, tag="xt", bufs=4)
                 for a in range(WORD_TILES):
                     first = t * (K // 2) + a * P
                     nc.tensor.transpose(xt[:, a, :], x_words[:, first : first + P], ident[:])
-                nc.scalar.copy(
+                copy_out = nc.vector.tensor_copy if t == T - 1 else nc.scalar.copy
+                copy_out(
                     out=grouped_words[:, :, t * P : (t + 1) * P, :],
                     in_=xt[:].rearrange("p (c u) n -> p c n u", c=PASSES),
                 )
@@ -226,7 +227,7 @@ def tile_fluxjointattention_pa_t_kernel(
         def transpose_back(g):
             for qk in range(2):
                 ybt = ybt_tiles[(g, qk)]
-                ybp = psum.tile([P, T, D], F32, tag="ybp", bufs=3)
+                ybp = psum.tile([P, T, D], F32, tag="ybp", bufs=2)
                 for t in range(T):
                     nc.tensor.transpose(ybp[:, t, :], ybt[:, t * P : (t + 1) * P], ident[:])
                 ybp_tiles[(g, qk)] = ybp
@@ -268,35 +269,36 @@ def tile_fluxjointattention_pa_t_kernel(
                             op1=ALU.mult,
                         )
                 result = work.tile([P, T, D], F32, tag="result", bufs=4)
-                nc.vector.tensor_tensor(out=result[:], in0=from_even[:], in1=from_odd[:], op=ALU.add)
+                nc.gpsimd.tensor_tensor(out=result[:], in0=from_even[:], in1=from_odd[:], op=ALU.add)
                 nc.sync.dma_start(
                     out=outs[qk][b, block * BLOCK : (block + 1) * BLOCK, 0, :].rearrange("(p t) d -> p t d", t=T),
                     in_=result[:],
                 )
 
-        for i in range(GROUPS + 3):
-            if i + LOOKAHEAD < GROUPS:
-                load_x(i + LOOKAHEAD)
-            if 0 <= i - 2 < GROUPS:
-                add_bias(i - 2)
-            if i < GROUPS:
-                transpose_x(i)
-            if i == 0:
-                spread_vectors()
-                quantise_weights(0)
-                for qk in range(2):
-                    build_tables(0, qk)
-            if i == 3:
-                quantise_weights(1)
-            if 0 <= i - 3 < GROUPS:
-                rotate_and_store(i - 3)
-            if i % BATCH < 2 and i // BATCH + 1 < BLOCKS:
-                build_tables(i // BATCH + 1, i % BATCH)
-            if 0 <= i - 2 < GROUPS:
-                transpose_back(i - 2)
-            if 0 <= i - 1 < GROUPS:
-                project(i - 1)
-            if i < GROUPS:
-                quantise_x(i)
-            if 0 <= i - 2 < GROUPS:
-                norms(i - 2)
+        with tc.manual_schedule():
+            for i in range(GROUPS + 3):
+                if i + LOOKAHEAD < GROUPS:
+                    load_x(i + LOOKAHEAD)
+                if 0 <= i - 3 < GROUPS:
+                    rotate_and_store(i - 3)
+                if 0 <= i - 2 < GROUPS:
+                    add_bias(i - 2)
+                if i < GROUPS:
+                    transpose_x(i)
+                if i == 0:
+                    spread_vectors()
+                    quantise_weights(0)
+                    for qk in range(2):
+                        build_tables(0, qk)
+                if i == 3:
+                    quantise_weights(1)
+                if i % BATCH < 2 and i // BATCH + 1 < BLOCKS:
+                    build_tables(i // BATCH + 1, i % BATCH)
+                if 0 <= i - 2 < GROUPS:
+                    transpose_back(i - 2)
+                if 0 <= i - 1 < GROUPS:
+                    project(i - 1)
+                if i < GROUPS:
+                    quantise_x(i)
+                if 0 <= i - 2 < GROUPS:
+                    norms(i - 2)

@@ -66,7 +66,6 @@ def tile_fluxjointattention_pa_t_kernel(
         yt_tiles = {}
         ybt_tiles = {}
         ybp_tiles = {}
-        r_tiles = {}
 
         def load_x(g):
             block, b = divmod(g, BATCH)
@@ -232,55 +231,46 @@ def tile_fluxjointattention_pa_t_kernel(
                     nc.tensor.transpose(ybp[:, t, :], ybt[:, t * P : (t + 1) * P], ident[:])
                 ybp_tiles[(g, qk)] = ybp
 
-        def norms(g):
-            ss = work.tile([P, 2 * T], F32, tag="ss", bufs=3)
-            for qk in range(2):
-                for t in range(T):
-                    squares = work.tile([P, D], F32, tag="squares", bufs=2)
-                    nc.scalar.activation(
-                        out=squares[:],
-                        in_=ybp_tiles[(g, qk)][:, t, :],
-                        func=ACT.Square,
-                        accum_out=ss[:, qk * T + t : qk * T + t + 1],
-                    )
-            rms = work.tile([P, 2 * T], F32, tag="rms", bufs=3)
-            nc.scalar.activation(out=rms[:], in_=ss[:], func=ACT.Sqrt, scale=1.0 / D, bias=EPS)
-            r = work.tile([P, 2 * T], F32, tag="r", bufs=3)
-            nc.vector.reciprocal(out=r[:], in_=rms[:])
-            r_tiles[g] = r
-
-        def rotate_and_store(g):
-            block, b = divmod(g, BATCH)
-            r = r_tiles[g]
-            for qk in range(2):
-                ybp = ybp_tiles[(g, qk)]
-                from_even = work.tile([P, T, D], F32, tag="from_even", bufs=4)
-                from_odd = work.tile([P, T, D], F32, tag="from_odd", bufs=4)
-                for t in range(T):
-                    col = qk * T + t
-                    pairs = ybp[:, t, :].rearrange("p (i h) -> p i h", h=2)
-                    for h, tabs, part in ((0, even_tabs, from_even), (1, odd_tabs, from_odd)):
-                        nc.vector.scalar_tensor_tensor(
-                            out=part[:, t, :].rearrange("p (i h) -> p i h", h=2),
-                            in0=pairs[:, :, h : h + 1].to_broadcast([P, HALF, 2]),
-                            scalar=r[:, col : col + 1],
-                            in1=tabs[(block, qk)][:, t, :, :].rearrange("p h i -> p i h"),
-                            op0=ALU.mult,
-                            op1=ALU.mult,
-                        )
-                result = work.tile([P, T, D], F32, tag="result", bufs=4)
-                nc.gpsimd.tensor_tensor(out=result[:], in0=from_even[:], in1=from_odd[:], op=ALU.add)
-                nc.sync.dma_start(
-                    out=outs[qk][b, block * BLOCK : (block + 1) * BLOCK, 0, :].rearrange("(p t) d -> p t d", t=T),
-                    in_=result[:],
+        def norm(g, qk):
+            ss = work.tile([P, T], F32, tag="ss", bufs=4)
+            for t in range(T):
+                squares = work.tile([P, D], F32, tag="squares", bufs=2)
+                nc.scalar.activation(
+                    out=squares[:], in_=ybp_tiles[(g, qk)][:, t, :], func=ACT.Square, accum_out=ss[:, t : t + 1]
                 )
+            rms = work.tile([P, T], F32, tag="rms", bufs=4)
+            nc.scalar.activation(out=rms[:], in_=ss[:], func=ACT.Sqrt, scale=1.0 / D, bias=EPS)
+            r = work.tile([P, T], F32, tag="r", bufs=4)
+            nc.vector.reciprocal(out=r[:], in_=rms[:])
+            return r
+
+        def rotate_and_store(g, qk, r):
+            block, b = divmod(g, BATCH)
+            ybp = ybp_tiles[(g, qk)]
+            from_even = work.tile([P, T, D], F32, tag="from_even", bufs=4)
+            from_odd = work.tile([P, T, D], F32, tag="from_odd", bufs=4)
+            for t in range(T):
+                pairs = ybp[:, t, :].rearrange("p (i h) -> p i h", h=2)
+                for h, tabs, part in ((0, even_tabs, from_even), (1, odd_tabs, from_odd)):
+                    nc.vector.scalar_tensor_tensor(
+                        out=part[:, t, :].rearrange("p (i h) -> p i h", h=2),
+                        in0=pairs[:, :, h : h + 1].to_broadcast([P, HALF, 2]),
+                        scalar=r[:, t : t + 1],
+                        in1=tabs[(block, qk)][:, t, :, :].rearrange("p h i -> p i h"),
+                        op0=ALU.mult,
+                        op1=ALU.mult,
+                    )
+            result = work.tile([P, T, D], F32, tag="result", bufs=4)
+            nc.gpsimd.tensor_tensor(out=result[:], in0=from_even[:], in1=from_odd[:], op=ALU.add)
+            nc.sync.dma_start(
+                out=outs[qk][b, block * BLOCK : (block + 1) * BLOCK, 0, :].rearrange("(p t) d -> p t d", t=T),
+                in_=result[:],
+            )
 
         with tc.manual_schedule():
-            for i in range(GROUPS + 3):
+            for i in range(GROUPS + 2):
                 if i + LOOKAHEAD < GROUPS:
                     load_x(i + LOOKAHEAD)
-                if 0 <= i - 3 < GROUPS:
-                    rotate_and_store(i - 3)
                 if 0 <= i - 2 < GROUPS:
                     add_bias(i - 2)
                 if i < GROUPS:
@@ -301,4 +291,5 @@ def tile_fluxjointattention_pa_t_kernel(
                 if i < GROUPS:
                     quantise_x(i)
                 if 0 <= i - 2 < GROUPS:
-                    norms(i - 2)
+                    for qk in range(2):
+                        rotate_and_store(i - 2, qk, norm(i - 2, qk))

@@ -24,6 +24,7 @@ GROUPS = BLOCKS * BATCH
 PASSES = K // 512
 WORD_TILES = K // 2 // P
 LOOKAHEAD = 4
+MATMUL_TILES = 2
 
 FLOPS = 2 * BATCH * BLOCKS * BLOCK * K * 2 * D
 
@@ -66,6 +67,7 @@ def tile_fluxjointattention_pa_t_kernel(
         yt_tiles = {}
         ybt_tiles = {}
         ybp_tiles = {}
+        rms_tiles = {}
 
         def load_x(g):
             block, b = divmod(g, BATCH)
@@ -171,11 +173,13 @@ def tile_fluxjointattention_pa_t_kernel(
             even_tabs[(block, qk)] = even_tab
             odd_tabs[(block, qk)] = odd_tab
 
-        def transpose_x(g):
+        def transpose_x(g, half):
             x_words = x_tiles[g][:].bitcast(F32)
-            grouped = work.tile([P, PASSES * BLOCK * 4], BF16, tag="grouped", bufs=2, align_bytes=64)
-            grouped_words = grouped[:].bitcast(F32).rearrange("p (c n u) -> p c n u", c=PASSES, u=2)
-            for t in range(T):
+            if half == 0:
+                grouped = work.tile([P, PASSES * BLOCK * 4], BF16, tag="grouped", bufs=2, align_bytes=64)
+                grouped_tiles[g] = grouped
+            grouped_words = grouped_tiles[g][:].bitcast(F32).rearrange("p (c n u) -> p c n u", c=PASSES, u=2)
+            for t in range(2 * half, 2 * half + 2):
                 xt = psum.tile([P, WORD_TILES, P], F32, tag="xt", bufs=4)
                 for a in range(WORD_TILES):
                     first = t * (K // 2) + a * P
@@ -185,7 +189,6 @@ def tile_fluxjointattention_pa_t_kernel(
                     out=grouped_words[:, :, t * P : (t + 1) * P, :],
                     in_=xt[:].rearrange("p (c u) n -> p c n u", c=PASSES),
                 )
-            grouped_tiles[g] = grouped
 
         def quantise_x(g):
             grouped = grouped_tiles[g]
@@ -194,42 +197,43 @@ def tile_fluxjointattention_pa_t_kernel(
             nc.vector.quantize_mx(out=codes[:].bitcast(FP8X4), scales=scales[:], in_=grouped[:])
             mx_tiles[g] = (codes, scales)
 
-        def project(g):
+        def project(g, qk):
             stream = min(g // BATCH, 1)
             codes, scales = mx_tiles[g]
-            for qk in range(2):
-                yt = psum.tile([P, BLOCK], F32, tag="yt", bufs=2)
-                for c in range(PASSES):
-                    w_cols = slice((2 * qk + c) * P, (2 * qk + c + 1) * P)
-                    x_cols = slice(c * BLOCK, (c + 1) * BLOCK)
-                    nc.tensor.matmul_mx(
-                        out=yt[:],
-                        lhsT=w_codes[stream][:, w_cols].bitcast(FP8X4),
-                        lhsT_scale=w_scales[stream][:, w_cols],
-                        rhs=codes[:, x_cols].bitcast(FP8X4),
-                        rhs_scale=scales[:, x_cols],
-                        start=(c == 0),
-                        stop=(c == PASSES - 1),
-                    )
-                yt_tiles[(g, qk)] = yt
-
-        def add_bias(g):
-            stream = min(g // BATCH, 1)
-            for qk in range(2):
-                ybt = work.tile([P, BLOCK], F32, tag="ybt", bufs=4)
-                j = 2 * stream + qk
-                nc.scalar.activation(
-                    out=ybt[:], in_=yt_tiles[(g, qk)][:], func=ACT.Identity, bias=bias_col[:, j : j + 1]
+            yt = psum.tile([P, BLOCK], F32, tag="yt", bufs=2)
+            for c in range(PASSES):
+                w_cols = slice((2 * qk + c) * P, (2 * qk + c + 1) * P)
+                x_cols = slice(c * BLOCK, (c + 1) * BLOCK)
+                nc.tensor.matmul_mx(
+                    out=yt[:],
+                    lhsT=w_codes[stream][:, w_cols].bitcast(FP8X4),
+                    lhsT_scale=w_scales[stream][:, w_cols],
+                    rhs=codes[:, x_cols].bitcast(FP8X4),
+                    rhs_scale=scales[:, x_cols],
+                    start=(c == 0),
+                    stop=(c == PASSES - 1),
                 )
-                ybt_tiles[(g, qk)] = ybt
+            yt_tiles[(g, qk)] = yt
 
-        def transpose_back(g):
-            for qk in range(2):
-                ybt = ybt_tiles[(g, qk)]
-                ybp = psum.tile([P, T, D], F32, tag="ybp", bufs=2)
-                for t in range(T):
-                    nc.tensor.transpose(ybp[:, t, :], ybt[:, t * P : (t + 1) * P], ident[:])
-                ybp_tiles[(g, qk)] = ybp
+        def add_bias(g, qk):
+            j = 2 * min(g // BATCH, 1) + qk
+            ybt = work.tile([P, BLOCK], F32, tag="ybt", bufs=4)
+            nc.scalar.activation(
+                out=ybt[:], in_=yt_tiles[(g, qk)][:], func=ACT.Identity, bias=bias_col[:, j : j + 1]
+            )
+            ybt_tiles[(g, qk)] = ybt
+
+        def bring_back_as_matmuls(g, qk):
+            ybp = psum.tile([P, T, D], F32, tag="ybp", bufs=2)
+            for t in range(MATMUL_TILES):
+                nc.tensor.matmul(
+                    out=ybp[:, t, :], lhsT=ybt_tiles[(g, qk)][:, t * P : (t + 1) * P], rhs=ident[:], start=True, stop=True
+                )
+            ybp_tiles[(g, qk)] = ybp
+
+        def bring_back_as_transposes(g, qk):
+            for t in range(MATMUL_TILES, T):
+                nc.tensor.transpose(ybp_tiles[(g, qk)][:, t, :], ybt_tiles[(g, qk)][:, t * P : (t + 1) * P], ident[:])
 
         def norm(g, qk):
             ss = work.tile([P, T], F32, tag="ss", bufs=4)
@@ -240,12 +244,12 @@ def tile_fluxjointattention_pa_t_kernel(
                 )
             rms = work.tile([P, T], F32, tag="rms", bufs=4)
             nc.scalar.activation(out=rms[:], in_=ss[:], func=ACT.Sqrt, scale=1.0 / D, bias=EPS)
-            r = work.tile([P, T], F32, tag="r", bufs=4)
-            nc.vector.reciprocal(out=r[:], in_=rms[:])
-            return r
+            rms_tiles[(g, qk)] = rms
 
-        def rotate_and_store(g, qk, r):
+        def rotate_and_store(g, qk):
             block, b = divmod(g, BATCH)
+            r = work.tile([P, T], F32, tag="r", bufs=4)
+            nc.vector.reciprocal(out=r[:], in_=rms_tiles[(g, qk)][:])
             ybp = ybp_tiles[(g, qk)]
             from_even = work.tile([P, T, D], F32, tag="from_even", bufs=4)
             from_odd = work.tile([P, T, D], F32, tag="from_odd", bufs=4)
@@ -267,29 +271,38 @@ def tile_fluxjointattention_pa_t_kernel(
                 in_=result[:],
             )
 
+        units = 2 * GROUPS
+
+        def unit(j):
+            return divmod(j, 2) if 0 <= j < units else None
+
         with tc.manual_schedule():
-            for i in range(GROUPS + 2):
-                if i + LOOKAHEAD < GROUPS:
-                    load_x(i + LOOKAHEAD)
-                if 0 <= i - 2 < GROUPS:
-                    add_bias(i - 2)
-                if i < GROUPS:
-                    transpose_x(i)
-                if i == 0:
+            for step in range(units + 5):
+                g, half = divmod(step, 2)
+                if half == 0 and g + LOOKAHEAD < GROUPS:
+                    load_x(g + LOOKAHEAD)
+                if unit(step - 5):
+                    rotate_and_store(*unit(step - 5))
+                if unit(step - 3):
+                    add_bias(*unit(step - 3))
+                if unit(step - 4):
+                    bring_back_as_matmuls(*unit(step - 4))
+                if g < GROUPS:
+                    transpose_x(g, half)
+                if step == 0:
                     spread_vectors()
                     quantise_weights(0)
                     for qk in range(2):
                         build_tables(0, qk)
-                if i == 3:
+                if step == 6:
                     quantise_weights(1)
-                if i % BATCH < 2 and i // BATCH + 1 < BLOCKS:
-                    build_tables(i // BATCH + 1, i % BATCH)
-                if 0 <= i - 2 < GROUPS:
-                    transpose_back(i - 2)
-                if 0 <= i - 1 < GROUPS:
-                    project(i - 1)
-                if i < GROUPS:
-                    quantise_x(i)
-                if 0 <= i - 2 < GROUPS:
-                    for qk in range(2):
-                        rotate_and_store(i - 2, qk, norm(i - 2, qk))
+                if half == 0 and g % BATCH < 2 and g // BATCH + 1 < BLOCKS:
+                    build_tables(g // BATCH + 1, g % BATCH)
+                if unit(step - 4):
+                    bring_back_as_transposes(*unit(step - 4))
+                if unit(step - 2):
+                    project(*unit(step - 2))
+                if half == 1 and g < GROUPS:
+                    quantise_x(g)
+                if unit(step - 4):
+                    norm(*unit(step - 4))

from contextlib import ExitStack

import concourse.mybir as mybir
from concourse.masks import make_identity

F32 = mybir.dt.float32
BF16 = mybir.dt.bfloat16
U32 = mybir.dt.uint32
U8 = mybir.dt.uint8
FP8X4 = mybir.dt.float8_e4m3fn_x4
ACT = mybir.ActivationFunctionType
ALU = mybir.AluOpType

P = 128
BATCH = 4
K = 1024
D = 128
HALF = D // 2
EPS = 1e-6
BLOCK = 512
T = BLOCK // P
BLOCKS = 4
GROUPS = BLOCKS * BATCH
PASSES = K // 512
WORD_TILES = K // 2 // P
LOOKAHEAD = 4
MATMUL_TILES = 2

FLOPS = 2 * BATCH * BLOCKS * BLOCK * K * 2 * D


def tile_fluxjointattention_pa_t_kernel(
    tc,
    hidden_states,
    encoder_hidden_states,
    rope_cos,
    rope_sin,
    Wq,
    Wk,
    Waq,
    Wak,
    bq,
    bk,
    baq,
    bak,
    g_q,
    g_k,
    g_aq,
    g_ak,
    out_0,
    out_1,
):
    nc = tc.nc
    outs = (out_0, out_1)
    weights = (Waq, Wak, Wq, Wk)
    biases = (baq, bak, bq, bk)
    gains = (g_aq, g_ak, g_q, g_k)

    with ExitStack() as ctx:
        consts = ctx.enter_context(tc.tile_pool(name="consts", bufs=1))
        work = ctx.enter_context(tc.tile_pool(name="work", bufs=2))
        psum = ctx.enter_context(tc.psum_pool(name="psum", bufs=1))

        x_tiles = {}
        grouped_tiles = {}
        mx_tiles = {}
        yt_tiles = {}
        ybt_tiles = {}
        ybp_tiles = {}
        rms_tiles = {}

        def load_x(g):
            block, b = divmod(g, BATCH)
            if block == 0:
                rows = encoder_hidden_states[b]
            else:
                rows = hidden_states[b, (block - 1) * BLOCK : block * BLOCK, :]
            x_sb = work.tile([P, T * K], BF16, tag="x", bufs=LOOKAHEAD + 2)
            nc.sync.dma_start(out=x_sb[:], in_=rows.rearrange("(p t) k -> p (t k)", t=T))
            x_tiles[g] = x_sb

        warm = consts.tile([P, 1], F32)
        nc.vector.memset(warm[:], 1.0)
        nc.scalar.activation(out=warm[:], in_=warm[:], func=ACT.Sqrt)

        bias_rows = consts.tile([P, P], BF16)
        nc.vector.memset(bias_rows[:], 0.0)
        gain_rows = consts.tile([P, 4 * D], BF16)
        nc.vector.memset(gain_rows[:], 0.0)
        ones = consts.tile([P, P], BF16)
        nc.vector.memset(ones[:], 1.0)

        ident = consts.tile([P, P], F32)
        make_identity(nc, ident[:])
        ident_bf = consts.tile([P, P], BF16)
        nc.vector.tensor_copy(out=ident_bf[:], in_=ident[:])

        w_raw = {}

        def load_weights(stream):
            raw = consts.tile([P, 2 * K * D // P], BF16, name="w_raw%d" % stream)
            for qk in range(2):
                nc.sync.dma_start(
                    out=raw[:, qk * 1024 : (qk + 1) * 1024].rearrange("p (a f) -> p a f", a=4),
                    in_=weights[2 * stream + qk].rearrange("(a p e) n -> p a (e n)", a=4, p=P, e=2),
                )
            w_raw[stream] = raw

        load_x(0)
        load_weights(0)
        for j in range(4):
            nc.sync.dma_start(out=bias_rows[j : j + 1, :], in_=biases[j].unsqueeze(0))
            nc.sync.dma_start(out=gain_rows[0:1, j * D : (j + 1) * D], in_=gains[j].unsqueeze(0))
        load_x(1)
        cos_sb = consts.tile([P, BLOCKS, T * D], BF16)
        nc.sync.dma_start(out=cos_sb[:], in_=rope_cos.rearrange("(c p t) d -> p c (t d)", c=BLOCKS, p=P, t=T))
        sin_sb = consts.tile([P, BLOCKS, T * D], BF16)
        nc.sync.dma_start(out=sin_sb[:], in_=rope_sin.rearrange("(c p t) d -> p c (t d)", c=BLOCKS, p=P, t=T))
        load_x(2)
        load_x(3)
        load_weights(1)

        w_codes = {}
        w_scales = {}

        def quantise_weights(stream):
            grouped = consts.tile([P, 2048], BF16, name="w_grouped%d" % stream, align_bytes=64)
            nc.vector.tensor_copy(
                out=grouped[:].rearrange("p (m n j) -> p m n j", m=4, j=4),
                in_=w_raw[stream][:].rearrange("p (m j n) -> p m n j", m=4, j=4),
            )
            codes = consts.tile([P, 512], U32, name="w_codes%d" % stream, align_bytes=64)
            scales = consts.tile([P, 512], U8, name="w_scales%d" % stream, align_bytes=64)
            nc.vector.quantize_mx(out=codes[:].bitcast(FP8X4), scales=scales[:], in_=grouped[:])
            w_codes[stream] = codes
            w_scales[stream] = scales

        bias_col = consts.tile([P, 4], F32)
        gain_pairs = consts.tile([P, 4, 3, HALF], F32)

        def spread_vectors():
            bias_ps = psum.tile([P, P], BF16, tag="ybp", bufs=2)
            nc.tensor.transpose(bias_ps[:], bias_rows[:], ident_bf[:])
            nc.vector.tensor_copy(out=bias_col[:], in_=bias_ps[:, 0:4])
            gain_ps = psum.tile([P, 4 * D], F32, tag="yt", bufs=2)
            nc.tensor.matmul(out=gain_ps[:], lhsT=ones[:], rhs=gain_rows[:], start=True, stop=True)
            nc.vector.tensor_copy(
                out=gain_pairs[:, :, 0:2, :], in_=gain_ps[:].rearrange("p (j i h) -> p j h i", j=4, h=2)
            )
            nc.vector.tensor_scalar_mul(out=gain_pairs[:, :, 2, :], in0=gain_pairs[:, :, 1, :], scalar1=-1.0)

        even_tabs = {}
        odd_tabs = {}

        def build_tables(block, qk):
            j = 2 * min(block, 1) + qk
            cos_pairs = cos_sb[:, block, :].rearrange("p (t i h) -> p t h i", t=T, h=2)
            sin_pairs = sin_sb[:, block, :].rearrange("p (t i h) -> p t h i", t=T, h=2)
            even_tab = consts.tile([P, T, 2, HALF], F32, name="even_tab%d_%d" % (block, qk))
            odd_tab = consts.tile([P, T, 2, HALF], F32, name="odd_tab%d_%d" % (block, qk))
            for table, h, angles, gain in (
                (even_tab, 0, cos_pairs, 0),
                (even_tab, 1, sin_pairs, 0),
                (odd_tab, 0, sin_pairs, 2),
                (odd_tab, 1, cos_pairs, 1),
            ):
                nc.gpsimd.tensor_tensor(
                    out=table[:, :, h, :],
                    in0=angles[:, :, h, :],
                    in1=gain_pairs[:, j, gain, :].unsqueeze(1).to_broadcast([P, T, HALF]),
                    op=ALU.mult,
                )
            even_tabs[(block, qk)] = even_tab
            odd_tabs[(block, qk)] = odd_tab

        def transpose_x(g, half):
            x_words = x_tiles[g][:].bitcast(F32)
            if half == 0:
                grouped = work.tile([P, PASSES * BLOCK * 4], BF16, tag="grouped", bufs=2, align_bytes=64)
                grouped_tiles[g] = grouped
            grouped_words = grouped_tiles[g][:].bitcast(F32).rearrange("p (c n u) -> p c n u", c=PASSES, u=2)
            for t in range(2 * half, 2 * half + 2):
                xt = psum.tile([P, WORD_TILES, P], F32, tag="xt", bufs=4)
                for a in range(WORD_TILES):
                    first = t * (K // 2) + a * P
                    nc.tensor.transpose(xt[:, a, :], x_words[:, first : first + P], ident[:])
                copy_out = nc.vector.tensor_copy if t == T - 1 else nc.scalar.copy
                copy_out(
                    out=grouped_words[:, :, t * P : (t + 1) * P, :],
                    in_=xt[:].rearrange("p (c u) n -> p c n u", c=PASSES),
                )

        def quantise_x(g):
            grouped = grouped_tiles[g]
            codes = work.tile([P, PASSES * BLOCK], U32, tag="codes", bufs=2, align_bytes=64)
            scales = work.tile([P, PASSES * BLOCK], U8, tag="scales", bufs=2, align_bytes=64)
            nc.vector.quantize_mx(out=codes[:].bitcast(FP8X4), scales=scales[:], in_=grouped[:])
            mx_tiles[g] = (codes, scales)

        def project(g, qk):
            stream = min(g // BATCH, 1)
            codes, scales = mx_tiles[g]
            yt = psum.tile([P, BLOCK], F32, tag="yt", bufs=2)
            for c in range(PASSES):
                w_cols = slice((2 * qk + c) * P, (2 * qk + c + 1) * P)
                x_cols = slice(c * BLOCK, (c + 1) * BLOCK)
                nc.tensor.matmul_mx(
                    out=yt[:],
                    lhsT=w_codes[stream][:, w_cols].bitcast(FP8X4),
                    lhsT_scale=w_scales[stream][:, w_cols],
                    rhs=codes[:, x_cols].bitcast(FP8X4),
                    rhs_scale=scales[:, x_cols],
                    start=(c == 0),
                    stop=(c == PASSES - 1),
                )
            yt_tiles[(g, qk)] = yt

        def add_bias(g, qk):
            j = 2 * min(g // BATCH, 1) + qk
            ybt = work.tile([P, BLOCK], F32, tag="ybt", bufs=4)
            nc.scalar.activation(
                out=ybt[:], in_=yt_tiles[(g, qk)][:], func=ACT.Identity, bias=bias_col[:, j : j + 1]
            )
            ybt_tiles[(g, qk)] = ybt

        def bring_back_as_matmuls(g, qk):
            ybp = psum.tile([P, T, D], F32, tag="ybp", bufs=2)
            for t in range(MATMUL_TILES):
                nc.tensor.matmul(
                    out=ybp[:, t, :], lhsT=ybt_tiles[(g, qk)][:, t * P : (t + 1) * P], rhs=ident[:], start=True, stop=True
                )
            ybp_tiles[(g, qk)] = ybp

        def bring_back_as_transposes(g, qk):
            for t in range(MATMUL_TILES, T):
                nc.tensor.transpose(ybp_tiles[(g, qk)][:, t, :], ybt_tiles[(g, qk)][:, t * P : (t + 1) * P], ident[:])

        def norm(g, qk):
            ss = work.tile([P, T], F32, tag="ss", bufs=4)
            for t in range(T):
                squares = work.tile([P, D], F32, tag="squares", bufs=2)
                nc.scalar.activation(
                    out=squares[:], in_=ybp_tiles[(g, qk)][:, t, :], func=ACT.Square, accum_out=ss[:, t : t + 1]
                )
            rms = work.tile([P, T], F32, tag="rms", bufs=4)
            nc.scalar.activation(out=rms[:], in_=ss[:], func=ACT.Sqrt, scale=1.0 / D, bias=EPS)
            rms_tiles[(g, qk)] = rms

        def rotate_and_store(g, qk):
            block, b = divmod(g, BATCH)
            r = work.tile([P, T], F32, tag="r", bufs=4)
            nc.vector.reciprocal(out=r[:], in_=rms_tiles[(g, qk)][:])
            ybp = ybp_tiles[(g, qk)]
            from_even = work.tile([P, T, D], F32, tag="from_even", bufs=4)
            from_odd = work.tile([P, T, D], F32, tag="from_odd", bufs=4)
            for t in range(T):
                pairs = ybp[:, t, :].rearrange("p (i h) -> p i h", h=2)
                for h, tabs, part in ((0, even_tabs, from_even), (1, odd_tabs, from_odd)):
                    nc.vector.scalar_tensor_tensor(
                        out=part[:, t, :].rearrange("p (i h) -> p i h", h=2),
                        in0=pairs[:, :, h : h + 1].to_broadcast([P, HALF, 2]),
                        scalar=r[:, t : t + 1],
                        in1=tabs[(block, qk)][:, t, :, :].rearrange("p h i -> p i h"),
                        op0=ALU.mult,
                        op1=ALU.mult,
                    )
            result = work.tile([P, T, D], F32, tag="result", bufs=4)
            nc.gpsimd.tensor_tensor(out=result[:], in0=from_even[:], in1=from_odd[:], op=ALU.add)
            nc.sync.dma_start(
                out=outs[qk][b, block * BLOCK : (block + 1) * BLOCK, 0, :].rearrange("(p t) d -> p t d", t=T),
                in_=result[:],
            )

        units = 2 * GROUPS

        def unit(j):
            return divmod(j, 2) if 0 <= j < units else None

        with tc.manual_schedule():
            for step in range(units + 5):
                g, half = divmod(step, 2)
                if half == 0 and g + LOOKAHEAD < GROUPS:
                    load_x(g + LOOKAHEAD)
                if unit(step - 5):
                    rotate_and_store(*unit(step - 5))
                if unit(step - 3):
                    add_bias(*unit(step - 3))
                if unit(step - 4):
                    bring_back_as_matmuls(*unit(step - 4))
                if g < GROUPS:
                    transpose_x(g, half)
                if step == 0:
                    spread_vectors()
                    quantise_weights(0)
                    for qk in range(2):
                        build_tables(0, qk)
                if step == 6:
                    quantise_weights(1)
                if half == 0 and g % BATCH < 2 and g // BATCH + 1 < BLOCKS:
                    build_tables(g // BATCH + 1, g % BATCH)
                if unit(step - 4):
                    bring_back_as_transposes(*unit(step - 4))
                if unit(step - 2):
                    project(*unit(step - 2))
                if half == 1 and g < GROUPS:
                    quantise_x(g)
                if unit(step - 4):
                    norm(*unit(step - 4))
